import numpy as np
import ml_dtypes


def mxq(x, axis, fmt="e4m3"):
    dtype, down = {"e4m3": (ml_dtypes.float8_e4m3fn, 7), "e5m2": (ml_dtypes.float8_e5m2, 14)}[fmt]
    v = np.moveaxis(np.asarray(x, np.float32).astype(ml_dtypes.bfloat16).astype(np.float64), axis, -1)
    blocks = v.reshape(v.shape[:-1] + (-1, 32))
    amax = np.abs(blocks).max(-1, keepdims=True)
    byte = np.maximum(np.where(amax > 0, np.frexp(amax)[1] - 1 + 127, 0) - down, 1)
    scale = np.exp2(byte - 127.0)
    codes = (blocks / scale).astype(np.float32).astype(dtype).astype(np.float64)
    return np.moveaxis((codes * scale).reshape(v.shape), -1, axis)


WIDE = False


def mx_kscale(k):
    if not WIDE:
        return np.ones(k)
    levels = np.array([10, -10, 5, -5, 0])
    a = np.random.permutation(np.resize(levels, k // 512 * 4)).reshape(k // 512, 4)
    idx = np.arange(k)
    return np.exp2(a[idx // 512, idx % 128 // 32])


BF16 = ml_dtypes.bfloat16


def bf(x):
    return np.asarray(x, np.float32).astype(BF16)


def f64(x):
    return np.asarray(x).astype(np.float64)


E2M1 = np.array([0.0, 0.5, 1.0, 1.5, 2.0, 3.0, 4.0, 6.0, -0.0, -0.5, -1.0, -1.5, -2.0, -3.0, -4.0, -6.0])


def pack_weight(w, fmt):
    k, n = w.shape
    w = f64(bf(w)).reshape(k // 32, 32, n)
    amax = np.abs(w).max(1)
    if fmt == "e4m3":
        byte = np.frexp(amax)[1] - 1 + 127 - 7
    else:
        mant, ex = np.frexp(amax / 6.0)
        byte = np.where(mant > 0.5, ex, ex - 1) + 127
    byte = np.clip(np.where(amax > 0, byte, 1), 1, 254)
    scaled = (w * np.exp2(127.0 - byte)[:, None, :]).reshape(k, n).astype(np.float32)
    by_word = np.ascontiguousarray(scaled.reshape(k // 512, 128, 4, n).transpose(0, 1, 3, 2))
    if fmt == "e4m3":
        words = by_word.astype(ml_dtypes.float8_e4m3fn).view(np.uint8)
    else:
        c = by_word.astype(ml_dtypes.float4_e2m1fn).view(np.uint8) & 0xF
        words = c[..., 0::2] | (c[..., 1::2] << 4)
    return np.ascontiguousarray(words), np.ascontiguousarray(byte.astype(np.uint8).reshape(k // 512, 16, n))


def unpack_weight(words, scales, fmt):
    g, p, n, _ = words.shape
    if fmt == "e4m3":
        vals = np.ascontiguousarray(words).view(ml_dtypes.float8_e4m3fn).astype(np.float64)
    else:
        nib = np.empty((g, p, n, 4), np.uint8)
        nib[..., 0::2] = words & 0xF
        nib[..., 1::2] = words >> 4
        vals = E2M1[nib]
    vals = vals * np.repeat(np.exp2(scales.astype(np.float64) - 127.0), 8, axis=1)[..., None]
    return vals.transpose(0, 1, 3, 2).reshape(g * 512, n)

def pack4(w):
    words, scales = pack_weight(w, "e2m1")
    return words.reshape(words.shape[0], 128, -1), scales


def unpack4(words, scales):
    return unpack_weight(words.reshape(words.shape[0], 128, -1, 2), scales, "e2m1")


N, C, H, W, CO, KS, ST = 4, 512, 34, 34, 128, 3, 1
KK = KS * KS
F = C * KK
RUN = np.lcm(KK, 32)


def im2col(x, k, s):
    n, c, h, w = x.shape
    ho = (h - k) // s + 1
    wo = (w - k) // s + 1
    cols = np.stack([x[:, :, i:i + s * (ho - 1) + 1:s, j:j + s * (wo - 1) + 1:s] for i in range(k) for j in range(k)], axis=2)
    cols = cols.transpose(1, 2, 0, 3, 4).reshape(c * k * k, n * ho * wo)
    return cols, (n, ho, wo)


def setup_inputs():
    sc = np.repeat(mx_kscale(F)[::RUN], RUN // KK)
    sf = np.repeat(sc, KK)
    x = bf(np.random.standard_normal((N, C, H, W)) * sc[None, :, None, None])
    weight = np.random.uniform(0.0, 1.0, (CO, F)) * 1.7 / np.sqrt(F) / sf[None, :]
    words, scales = pack4(np.ascontiguousarray(weight.T))
    bias = bf(np.random.uniform(-1.0, 1.0, (CO, 1)) * 0.5)
    return {"x": x, "weight_words": words, "weight_scales": scales, "bias": bias}


def reference(x, weight_words, weight_scales, bias):
    cols, (n, ho, wo) = im2col(f64(x), KS, ST)
    flat = (unpack4(weight_words, weight_scales).T @ mxq(cols, 0, "e4m3")) + f64(bias)
    return flat.reshape(CO, n, ho, wo).transpose(1, 0, 2, 3)

@@ -1,0 +1,148 @@
+import concourse.mybir as mybir
+
+BF16 = mybir.dt.bfloat16
+F32 = mybir.dt.float32
+I32 = mybir.dt.int32
+U8 = mybir.dt.uint8
+U32 = mybir.dt.uint32
+FP8X4 = mybir.dt.float8_e4m3fn_x4
+FP4X4 = mybir.dt.float4_e2m1fn_x4
+
+IMAGES = 4
+CHANNELS = 512
+SIDE = 34
+KERNEL = 3
+OUT_SIDE = SIDE - KERNEL + 1
+OUT_CHANNELS = 128
+TAPS = KERNEL * KERNEL
+PLANE = SIDE * SIDE
+
+P = 128
+PACK = 4
+BLOCK_WORDS = 8
+RUN_K = 288
+RUN_CHANNELS = RUN_K // TAPS
+RUNS = CHANNELS // RUN_CHANNELS
+PASSES = RUN_K // (BLOCK_WORDS * PACK)
+RUN_ELEMENTS = RUN_CHANNELS * PLANE
+
+ROW = (OUT_SIDE - 1) * SIDE + OUT_SIDE
+ROW_PITCH = OUT_SIDE * SIDE
+POSITIONS = OUT_SIDE * OUT_SIDE
+N_TILE = 512
+
+VECTOR_ROWS = 16
+
+FLOPS = 2 * CHANNELS * TAPS * IMAGES * POSITIONS * OUT_CHANNELS
+
+
+def row_start(k_in_run):
+    channel, tap = divmod(k_in_run, TAPS)
+    kernel_row, kernel_column = divmod(tap, KERNEL)
+    return channel * PLANE + kernel_row * SIDE + kernel_column
+
+
+def two_rows(x_runs, first, second):
+    gap = second - first
+    window = min(first, RUN_ELEMENTS - 2 * gap)
+    lead = first - window
+    halves = x_runs[:, window : window + 2 * gap].rearrange("s (e d) -> s e d", e=2)
+    return halves[:, :, lead : lead + ROW]
+
+
+def tile_sparseconv2d_kernel(tc, x, weight_words, weight_scales, bias, out):
+    nc = tc.nc
+    with (
+        tc.tile_pool(name="keep", bufs=1) as keep,
+        tc.tile_pool(name="rows", bufs=4) as rows,
+        tc.tile_pool(name="quantised", bufs=3) as quantised,
+        tc.tile_pool(name="results", bufs=4) as results,
+        tc.psum_pool(name="sums", bufs=2) as sums,
+    ):
+        w_words = keep.tile([P, PASSES, 2 * OUT_CHANNELS], U8, align_bytes=64)
+        w_scales = keep.tile([P, PASSES, OUT_CHANNELS], U8, align_bytes=64)
+        nc.vector.memset(w_scales[:].rearrange("p b o -> p (b o)").bitcast(I32), 0)
+
+        word_rows = (
+            weight_words.rearrange("g p w -> (g p) w")
+            .bitcast(I32)
+            .rearrange("(s b r) w -> b s r w", b=PASSES, r=BLOCK_WORDS)
+        )
+        scale_rows = (
+            weight_scales.rearrange("g q o -> (g q) o").rearrange("(s b) o -> s (b o)", b=PASSES).bitcast(I32)
+        )
+
+        bias_bf16 = keep.tile([P, 1], BF16)
+        bias_f32 = keep.tile([P, 1], F32)
+
+        def load_weight():
+            for quadrant in range(4):
+                nc.sync.dma_start(
+                    out=w_scales[32 * quadrant : 32 * quadrant + 4].rearrange("p b o -> p (b o)").bitcast(I32),
+                    in_=scale_rows[4 * quadrant : 4 * quadrant + 4, :],
+                )
+            for b in range(PASSES):
+                nc.sync.dma_start(out=w_words[:, b, :].bitcast(I32), in_=word_rows[b])
+            nc.sync.dma_start(out=bias_bf16[:], in_=bias)
+            nc.vector.tensor_copy(out=bias_f32[:], in_=bias_bf16[:])
+
+        for n in range(IMAGES):
+            x_runs = x[n].rearrange("(s c) h w -> s (c h w)", c=RUN_CHANNELS)
+            out_rows = out[n].rearrange("o p q -> o (p q)")
+            acc = [sums.tile([OUT_CHANNELS, N_TILE], F32, name="acc%d" % half) for half in range(POSITIONS // N_TILE)]
+
+            for b in range(PASSES):
+                raw = rows.tile([P, PACK, ROW_PITCH], BF16)
+                for t in range(PACK):
+                    for r in range(BLOCK_WORDS // 2):
+                        k_first = BLOCK_WORDS * PACK * b + PACK * r + t
+                        k_second = k_first + PACK * (BLOCK_WORDS // 2)
+                        nc.sync.dma_start(
+                            out=raw[r : P : BLOCK_WORDS // 2, t, 0:ROW],
+                            in_=two_rows(x_runs, row_start(k_first), row_start(k_second)),
+                        )
+                if n == 0 and b == 0:
+                    load_weight()
+
+                grouped = rows.tile([P, POSITIONS, PACK], BF16, align_bytes=64)
+                raw_image = raw[:].rearrange("p t (h w) -> p t h w", w=SIDE)[:, :, :, 0:OUT_SIDE]
+                grouped_image = grouped[:].rearrange("p (h w) t -> p h w t", w=OUT_SIDE)
+                nc.vector.tensor_copy(
+                    out=grouped_image[:, 0:VECTOR_ROWS].rearrange("p h (c i) t -> p h c t i", i=PACK),
+                    in_=raw_image[:, :, 0:VECTOR_ROWS].rearrange("p t h (c i) -> p h c t i", i=PACK),
+                )
+                nc.scalar.copy(
+                    out=grouped_image[:, VECTOR_ROWS:OUT_SIDE],
+                    in_=raw_image[:, :, VECTOR_ROWS:OUT_SIDE].rearrange("p t h w -> p h w t"),
+                )
+
+                codes = quantised.tile([P, POSITIONS], U32, align_bytes=64)
+                scales = quantised.tile([P, POSITIONS], U8, align_bytes=64)
+                nc.vector.quantize_mx(
+                    out=codes[:].bitcast(FP8X4),
+                    scales=scales[:],
+                    in_=grouped[:].rearrange("p w t -> p (w t)"),
+                )
+
+                for half in range(POSITIONS // N_TILE):
+                    columns = slice(half * N_TILE, (half + 1) * N_TILE)
+                    nc.tensor.matmul_mx(
+                        out=acc[half][:],
+                        lhsT=w_words[:, b, :].bitcast(FP4X4),
+                        lhsT_scale=w_scales[:, b, :],
+                        rhs=codes[:, columns].bitcast(FP8X4),
+                        rhs_scale=scales[:, columns],
+                        start=(b == 0),
+                        stop=(b == PASSES - 1),
+                    )
+
+            for half in range(POSITIONS // N_TILE):
+                columns = slice(half * N_TILE, (half + 1) * N_TILE)
+                result = results.tile([OUT_CHANNELS, N_TILE], F32)
+                nc.scalar.activation(
+                    out=result[:],
+                    in_=acc[half][:],
+                    func=mybir.ActivationFunctionType.Identity,
+                    bias=bias_f32[:, 0:1],
+                )
+                nc.scalar.dma_start(out=out_rows[:, columns], in_=result[:])

@@ -24,14 +24,13 @@ RUN_K = 288
 RUN_CHANNELS = RUN_K // TAPS
 RUNS = CHANNELS // RUN_CHANNELS
 PASSES = RUN_K // (BLOCK_WORDS * PACK)
-RUN_ELEMENTS = RUN_CHANNELS * PLANE
 
 ROW = (OUT_SIDE - 1) * SIDE + OUT_SIDE
 ROW_PITCH = OUT_SIDE * SIDE
 POSITIONS = OUT_SIDE * OUT_SIDE
 N_TILE = 512
 
-VECTOR_ROWS = 16
+VECTOR_ROWS = 18
 
 FLOPS = 2 * CHANNELS * TAPS * IMAGES * POSITIONS * OUT_CHANNELS
 
@@ -42,22 +41,15 @@ def row_start(k_in_run):
     return channel * PLANE + kernel_row * SIDE + kernel_column
 
 
-def two_rows(x_runs, first, second):
-    gap = second - first
-    window = min(first, RUN_ELEMENTS - 2 * gap)
-    lead = first - window
-    halves = x_runs[:, window : window + 2 * gap].rearrange("s (e d) -> s e d", e=2)
-    return halves[:, :, lead : lead + ROW]
-
-
 def tile_sparseconv2d_kernel(tc, x, weight_words, weight_scales, bias, out):
     nc = tc.nc
     with (
         tc.tile_pool(name="keep", bufs=1) as keep,
-        tc.tile_pool(name="rows", bufs=4) as rows,
+        tc.tile_pool(name="rows", bufs=3) as rows,
+        tc.tile_pool(name="groups", bufs=3) as groups,
         tc.tile_pool(name="quantised", bufs=3) as quantised,
         tc.tile_pool(name="results", bufs=4) as results,
-        tc.psum_pool(name="sums", bufs=2) as sums,
+        tc.psum_pool(name="sums", bufs=1) as sums,
     ):
         w_words = keep.tile([P, PASSES, 2 * OUT_CHANNELS], U8, align_bytes=64)
         w_scales = keep.tile([P, PASSES, OUT_CHANNELS], U8, align_bytes=64)
@@ -86,26 +78,29 @@ def tile_sparseconv2d_kernel(tc, x, weight_words, weight_scales, bias, out):
             nc.sync.dma_start(out=bias_bf16[:], in_=bias)
             nc.vector.tensor_copy(out=bias_f32[:], in_=bias_bf16[:])
 
-        for n in range(IMAGES):
-            x_runs = x[n].rearrange("(s c) h w -> s (c h w)", c=RUN_CHANNELS)
-            out_rows = out[n].rearrange("o p q -> o (p q)")
-            acc = [sums.tile([OUT_CHANNELS, N_TILE], F32, name="acc%d" % half) for half in range(POSITIONS // N_TILE)]
+        x_runs = x.rearrange("n (s c) h w -> s n (c h w)", c=RUN_CHANNELS)
+        halves = POSITIONS // N_TILE
+        acc = [
+            [sums.tile([OUT_CHANNELS, N_TILE], F32, name="acc%d_%d" % (n, half)) for half in range(halves)]
+            for n in range(IMAGES)
+        ]
 
-            for b in range(PASSES):
-                raw = rows.tile([P, PACK, ROW_PITCH], BF16)
-                for t in range(PACK):
-                    for r in range(BLOCK_WORDS // 2):
-                        k_first = BLOCK_WORDS * PACK * b + PACK * r + t
-                        k_second = k_first + PACK * (BLOCK_WORDS // 2)
+        for b in range(PASSES):
+            raw = rows.tile([P, PACK, IMAGES, ROW_PITCH], BF16)
+            for t in range(PACK):
+                for r_low in range(BLOCK_WORDS // 2):
+                    for r in (r_low, r_low + BLOCK_WORDS // 2):
+                        start = row_start(BLOCK_WORDS * PACK * b + PACK * r + t)
                         nc.sync.dma_start(
-                            out=raw[r : P : BLOCK_WORDS // 2, t, 0:ROW],
-                            in_=two_rows(x_runs, row_start(k_first), row_start(k_second)),
+                            out=raw[r : P : BLOCK_WORDS, t, :, 0:ROW],
+                            in_=x_runs[:, :, start : start + ROW],
                         )
-                if n == 0 and b == 0:
-                    load_weight()
+            if b == 0:
+                load_weight()
 
-                grouped = rows.tile([P, POSITIONS, PACK], BF16, align_bytes=64)
-                raw_image = raw[:].rearrange("p t (h w) -> p t h w", w=SIDE)[:, :, :, 0:OUT_SIDE]
+            for n in range(IMAGES):
+                grouped = groups.tile([P, POSITIONS, PACK], BF16, align_bytes=64)
+                raw_image = raw[:, :, n, :].rearrange("p t (h w) -> p t h w", w=SIDE)[:, :, :, 0:OUT_SIDE]
                 grouped_image = grouped[:].rearrange("p (h w) t -> p h w t", w=OUT_SIDE)
                 nc.vector.tensor_copy(
                     out=grouped_image[:, 0:VECTOR_ROWS].rearrange("p h (c i) t -> p h c t i", i=PACK),
@@ -124,10 +119,10 @@ def tile_sparseconv2d_kernel(tc, x, weight_words, weight_scales, bias, out):
                     in_=grouped[:].rearrange("p w t -> p (w t)"),
                 )
 
-                for half in range(POSITIONS // N_TILE):
+                for half in range(halves):
                     columns = slice(half * N_TILE, (half + 1) * N_TILE)
                     nc.tensor.matmul_mx(
-                        out=acc[half][:],
+                        out=acc[n][half][:],
                         lhsT=w_words[:, b, :].bitcast(FP4X4),
                         lhsT_scale=w_scales[:, b, :],
                         rhs=codes[:, columns].bitcast(FP8X4),
@@ -136,12 +131,14 @@ def tile_sparseconv2d_kernel(tc, x, weight_words, weight_scales, bias, out):
                         stop=(b == PASSES - 1),
                     )
 
-            for half in range(POSITIONS // N_TILE):
+        for n in range(IMAGES):
+            out_rows = out[n].rearrange("o p q -> o (p q)")
+            for half in range(halves):
                 columns = slice(half * N_TILE, (half + 1) * N_TILE)
                 result = results.tile([OUT_CHANNELS, N_TILE], F32)
                 nc.scalar.activation(
                     out=result[:],
-                    in_=acc[half][:],
+                    in_=acc[n][half][:],
                     func=mybir.ActivationFunctionType.Identity,
                     bias=bias_f32[:, 0:1],
                 )

@@ -30,7 +30,9 @@ ROW_PITCH = OUT_SIDE * SIDE
 POSITIONS = OUT_SIDE * OUT_SIDE
 N_TILE = 512
 
-VECTOR_ROWS = 18
+VECTOR_ROWS = 20
+
+AHEAD = 2
 
 FLOPS = 2 * CHANNELS * TAPS * IMAGES * POSITIONS * OUT_CHANNELS
 
@@ -84,62 +86,80 @@ def tile_sparseconv2d_kernel(tc, x, weight_words, weight_scales, bias, out):
             [sums.tile([OUT_CHANNELS, N_TILE], F32, name="acc%d_%d" % (n, half)) for half in range(halves)]
             for n in range(IMAGES)
         ]
+        raw_of_pass = {}
 
-        for b in range(PASSES):
-            raw = rows.tile([P, PACK, IMAGES, ROW_PITCH], BF16)
-            for t in range(PACK):
-                for r_low in range(BLOCK_WORDS // 2):
-                    for r in (r_low, r_low + BLOCK_WORDS // 2):
-                        start = row_start(BLOCK_WORDS * PACK * b + PACK * r + t)
-                        nc.sync.dma_start(
-                            out=raw[r : P : BLOCK_WORDS, t, :, 0:ROW],
-                            in_=x_runs[:, :, start : start + ROW],
-                        )
-            if b == 0:
-                load_weight()
-
-            for n in range(IMAGES):
-                grouped = groups.tile([P, POSITIONS, PACK], BF16, align_bytes=64)
-                raw_image = raw[:, :, n, :].rearrange("p t (h w) -> p t h w", w=SIDE)[:, :, :, 0:OUT_SIDE]
-                grouped_image = grouped[:].rearrange("p (h w) t -> p h w t", w=OUT_SIDE)
-                nc.vector.tensor_copy(
-                    out=grouped_image[:, 0:VECTOR_ROWS].rearrange("p h (c i) t -> p h c t i", i=PACK),
-                    in_=raw_image[:, :, 0:VECTOR_ROWS].rearrange("p t h (c i) -> p h c t i", i=PACK),
-                )
-                nc.scalar.copy(
-                    out=grouped_image[:, VECTOR_ROWS:OUT_SIDE],
-                    in_=raw_image[:, :, VECTOR_ROWS:OUT_SIDE].rearrange("p t h w -> p h w t"),
+        def load_rows(b, t):
+            for r in range(BLOCK_WORDS):
+                queue = nc.sync if r < BLOCK_WORDS // 2 else nc.scalar
+                start = row_start(BLOCK_WORDS * PACK * b + PACK * r + t)
+                queue.dma_start(
+                    out=raw_of_pass[b][r : P : BLOCK_WORDS, t, :, 0:ROW],
+                    in_=x_runs[:, :, start : start + ROW],
                 )
 
-                codes = quantised.tile([P, POSITIONS], U32, align_bytes=64)
-                scales = quantised.tile([P, POSITIONS], U8, align_bytes=64)
-                nc.vector.quantize_mx(
-                    out=codes[:].bitcast(FP8X4),
-                    scales=scales[:],
-                    in_=grouped[:].rearrange("p w t -> p (w t)"),
-                )
+        def regroup(b, n):
+            grouped = groups.tile([P, POSITIONS, PACK], BF16, align_bytes=64, name="grouped")
+            raw_image = raw_of_pass[b][:, :, n, :].rearrange("p t (h w) -> p t h w", w=SIDE)[:, :, :, 0:OUT_SIDE]
+            grouped_image = grouped[:].rearrange("p (h w) t -> p h w t", w=OUT_SIDE)
+            nc.vector.tensor_copy(
+                out=grouped_image[:, 0:VECTOR_ROWS].rearrange("p h (c i) t -> p h c t i", i=PACK),
+                in_=raw_image[:, :, 0:VECTOR_ROWS].rearrange("p t h (c i) -> p h c t i", i=PACK),
+            )
+            nc.scalar.copy(
+                out=grouped_image[:, VECTOR_ROWS:OUT_SIDE],
+                in_=raw_image[:, :, VECTOR_ROWS:OUT_SIDE].rearrange("p t h w -> p h w t"),
+            )
+            return grouped
 
-                for half in range(halves):
-                    columns = slice(half * N_TILE, (half + 1) * N_TILE)
-                    nc.tensor.matmul_mx(
-                        out=acc[n][half][:],
-                        lhsT=w_words[:, b, :].bitcast(FP4X4),
-                        lhsT_scale=w_scales[:, b, :],
-                        rhs=codes[:, columns].bitcast(FP8X4),
-                        rhs_scale=scales[:, columns],
-                        start=(b == 0),
-                        stop=(b == PASSES - 1),
-                    )
-
-        for n in range(IMAGES):
-            out_rows = out[n].rearrange("o p q -> o (p q)")
+        def quantise_and_multiply(b, n, grouped):
+            codes = quantised.tile([P, POSITIONS], U32, align_bytes=64, name="codes")
+            scales = quantised.tile([P, POSITIONS], U8, align_bytes=64, name="scales")
+            nc.vector.quantize_mx(
+                out=codes[:].bitcast(FP8X4),
+                scales=scales[:],
+                in_=grouped[:].rearrange("p w t -> p (w t)"),
+            )
             for half in range(halves):
                 columns = slice(half * N_TILE, (half + 1) * N_TILE)
-                result = results.tile([OUT_CHANNELS, N_TILE], F32)
-                nc.scalar.activation(
-                    out=result[:],
-                    in_=acc[n][half][:],
-                    func=mybir.ActivationFunctionType.Identity,
-                    bias=bias_f32[:, 0:1],
+                nc.tensor.matmul_mx(
+                    out=acc[n][half][:],
+                    lhsT=w_words[:, b, :].bitcast(FP4X4),
+                    lhsT_scale=w_scales[:, b, :],
+                    rhs=codes[:, columns].bitcast(FP8X4),
+                    rhs_scale=scales[:, columns],
+                    start=(b == 0),
+                    stop=(b == PASSES - 1),
                 )
-                nc.scalar.dma_start(out=out_rows[:, columns], in_=result[:])
+            if b == PASSES - 1:
+                out_rows = out[n].rearrange("o p q -> o (p q)")
+                for half in range(halves):
+                    columns = slice(half * N_TILE, (half + 1) * N_TILE)
+                    result = results.tile([OUT_CHANNELS, N_TILE], F32, name="result")
+                    nc.scalar.activation(
+                        out=result[:],
+                        in_=acc[n][half][:],
+                        func=mybir.ActivationFunctionType.Identity,
+                        bias=bias_f32[:, 0:1],
+                    )
+                    nc.sync.dma_start(out=out_rows[:, columns], in_=result[:])
+
+        assert IMAGES == PACK
+        with tc.manual_schedule():
+            for b in range(AHEAD):
+                raw_of_pass[b] = rows.tile([P, PACK, IMAGES, ROW_PITCH], BF16, name="raw")
+                for t in range(PACK):
+                    load_rows(b, t)
+                if b == 0:
+                    load_weight()
+            previous = None
+            for b in range(PASSES):
+                for n in range(IMAGES):
+                    if b + AHEAD < PASSES:
+                        if n == 0:
+                            raw_of_pass[b + AHEAD] = rows.tile([P, PACK, IMAGES, ROW_PITCH], BF16, name="raw")
+                        load_rows(b + AHEAD, n)
+                    current = (b, n, regroup(b, n))
+                    if previous is not None:
+                        quantise_and_multiply(*previous)
+                    previous = current
+            quantise_and_multiply(*previous)

@@ -19,26 +19,30 @@ PLANE = SIDE * SIDE
 
 P = 128
 PACK = 4
-BLOCK_WORDS = 8
-RUN_K = 288
-RUN_CHANNELS = RUN_K // TAPS
-RUNS = CHANNELS // RUN_CHANNELS
-PASSES = RUN_K // (BLOCK_WORDS * PACK)
+WORDS = 2
+BLOCK_K = 32
+GROUP_CHANNELS = 8
+GROUP_K = GROUP_CHANNELS * TAPS
+GROUPS = CHANNELS // GROUP_CHANNELS
+STEPS = GROUP_K // (WORDS * PACK)
+QUARTERS = BLOCK_K // (WORDS * PACK)
+RUNS = GROUPS // QUARTERS
+RUN_BLOCKS = QUARTERS * GROUP_K // BLOCK_K
 
 ROW = (OUT_SIDE - 1) * SIDE + OUT_SIDE
 ROW_PITCH = OUT_SIDE * SIDE
 POSITIONS = OUT_SIDE * OUT_SIDE
 N_TILE = 512
+HALVES = POSITIONS // N_TILE
+TOGETHER = 2
 
-VECTOR_ROWS = 20
-
-AHEAD = 2
+VECTOR_ROWS = 18
 
 FLOPS = 2 * CHANNELS * TAPS * IMAGES * POSITIONS * OUT_CHANNELS
 
 
-def row_start(k_in_run):
-    channel, tap = divmod(k_in_run, TAPS)
+def row_start(k_in_group):
+    channel, tap = divmod(k_in_group, TAPS)
     kernel_row, kernel_column = divmod(tap, KERNEL)
     return channel * PLANE + kernel_row * SIDE + kernel_column
 
@@ -47,25 +51,25 @@ def tile_sparseconv2d_kernel(tc, x, weight_words, weight_scales, bias, out):
     nc = tc.nc
     with (
         tc.tile_pool(name="keep", bufs=1) as keep,
-        tc.tile_pool(name="rows", bufs=3) as rows,
-        tc.tile_pool(name="groups", bufs=3) as groups,
-        tc.tile_pool(name="quantised", bufs=3) as quantised,
+        tc.tile_pool(name="rows", bufs=4) as rows,
+        tc.tile_pool(name="groups", bufs=4) as groups,
+        tc.tile_pool(name="quantised", bufs=4) as quantised,
         tc.tile_pool(name="results", bufs=4) as results,
-        tc.psum_pool(name="sums", bufs=1) as sums,
+        tc.psum_pool(name="sums", bufs=2) as sums,
     ):
-        w_words = keep.tile([P, PASSES, 2 * OUT_CHANNELS], U8, align_bytes=64)
-        w_scales = keep.tile([P, PASSES, OUT_CHANNELS], U8, align_bytes=64)
+        w_words = keep.tile([P, QUARTERS, STEPS, 2 * OUT_CHANNELS], U8, align_bytes=64)
+        nc.vector.memset(w_words[:].rearrange("p g z w -> p (g z w)").bitcast(I32), 0)
+        w_scales = keep.tile([P, RUN_BLOCKS, OUT_CHANNELS], U8, align_bytes=64)
         nc.vector.memset(w_scales[:].rearrange("p b o -> p (b o)").bitcast(I32), 0)
 
         word_rows = (
-            weight_words.rearrange("g p w -> (g p) w")
+            weight_words.rearrange("a p w -> (a p) w")
             .bitcast(I32)
-            .rearrange("(s b r) w -> b s r w", b=PASSES, r=BLOCK_WORDS)
+            .rearrange("(s g z e) w -> g e s z w", g=QUARTERS, z=STEPS, e=WORDS)
         )
         scale_rows = (
-            weight_scales.rearrange("g q o -> (g q) o").rearrange("(s b) o -> s (b o)", b=PASSES).bitcast(I32)
+            weight_scales.rearrange("a q o -> (a q) o").rearrange("(s b) o -> s (b o)", b=RUN_BLOCKS).bitcast(I32)
         )
-
         bias_bf16 = keep.tile([P, 1], BF16)
         bias_f32 = keep.tile([P, 1], F32)
 
@@ -75,91 +79,78 @@ def tile_sparseconv2d_kernel(tc, x, weight_words, weight_scales, bias, out):
                     out=w_scales[32 * quadrant : 32 * quadrant + 4].rearrange("p b o -> p (b o)").bitcast(I32),
                     in_=scale_rows[4 * quadrant : 4 * quadrant + 4, :],
                 )
-            for b in range(PASSES):
-                nc.sync.dma_start(out=w_words[:, b, :].bitcast(I32), in_=word_rows[b])
+            for g in range(QUARTERS):
+                for e in range(WORDS):
+                    nc.sync.dma_start(
+                        out=w_words[WORDS * g + e : P : WORDS * QUARTERS, g, :, :].bitcast(I32),
+                        in_=word_rows[g, e],
+                    )
             nc.sync.dma_start(out=bias_bf16[:], in_=bias)
             nc.vector.tensor_copy(out=bias_f32[:], in_=bias_bf16[:])
 
-        x_runs = x.rearrange("n (s c) h w -> s n (c h w)", c=RUN_CHANNELS)
-        halves = POSITIONS // N_TILE
-        acc = [
-            [sums.tile([OUT_CHANNELS, N_TILE], F32, name="acc%d_%d" % (n, half)) for half in range(halves)]
-            for n in range(IMAGES)
-        ]
-        raw_of_pass = {}
+        x_groups = x.rearrange("n (u c) h w -> u n (c h w)", c=GROUP_CHANNELS)
 
-        def load_rows(b, t):
-            for r in range(BLOCK_WORDS):
-                queue = nc.sync if r < BLOCK_WORDS // 2 else nc.scalar
-                start = row_start(BLOCK_WORDS * PACK * b + PACK * r + t)
-                queue.dma_start(
-                    out=raw_of_pass[b][r : P : BLOCK_WORDS, t, :, 0:ROW],
-                    in_=x_runs[:, :, start : start + ROW],
-                )
+        for first_image in range(0, IMAGES, TOGETHER):
+            acc = [
+                [sums.tile([OUT_CHANNELS, N_TILE], F32, name="acc%d_%d" % (i, half)) for half in range(HALVES)]
+                for i in range(TOGETHER)
+            ]
+            for z in range(STEPS):
+                raw = rows.tile([P, PACK, TOGETHER, ROW_PITCH], BF16)
+                for t in range(PACK):
+                    for e in range(WORDS):
+                        start = row_start(WORDS * PACK * z + PACK * e + t)
+                        nc.sync.dma_start(
+                            out=raw[e:P:WORDS, t, :, 0:ROW],
+                            in_=x_groups[:, first_image : first_image + TOGETHER, start : start + ROW],
+                        )
+                if first_image == 0 and z == 0:
+                    load_weight()
 
-        def regroup(b, n):
-            grouped = groups.tile([P, POSITIONS, PACK], BF16, align_bytes=64, name="grouped")
-            raw_image = raw_of_pass[b][:, :, n, :].rearrange("p t (h w) -> p t h w", w=SIDE)[:, :, :, 0:OUT_SIDE]
-            grouped_image = grouped[:].rearrange("p (h w) t -> p h w t", w=OUT_SIDE)
-            nc.vector.tensor_copy(
-                out=grouped_image[:, 0:VECTOR_ROWS].rearrange("p h (c i) t -> p h c t i", i=PACK),
-                in_=raw_image[:, :, 0:VECTOR_ROWS].rearrange("p t h (c i) -> p h c t i", i=PACK),
-            )
-            nc.scalar.copy(
-                out=grouped_image[:, VECTOR_ROWS:OUT_SIDE],
-                in_=raw_image[:, :, VECTOR_ROWS:OUT_SIDE].rearrange("p t h w -> p h w t"),
-            )
-            return grouped
+                for i in range(TOGETHER):
+                    grouped = groups.tile([P, POSITIONS, PACK], BF16, align_bytes=64)
+                    raw_image = raw[:, :, i, :].rearrange("p t (h w) -> p t h w", w=SIDE)[:, :, :, 0:OUT_SIDE]
+                    grouped_image = grouped[:].rearrange("p (h w) t -> p h w t", w=OUT_SIDE)
+                    nc.vector.tensor_copy(
+                        out=grouped_image[:, 0:VECTOR_ROWS].rearrange("p h (c i) t -> p h c t i", i=PACK),
+                        in_=raw_image[:, :, 0:VECTOR_ROWS].rearrange("p t h (c i) -> p h c t i", i=PACK),
+                    )
+                    nc.scalar.copy(
+                        out=grouped_image[:, VECTOR_ROWS:OUT_SIDE],
+                        in_=raw_image[:, :, VECTOR_ROWS:OUT_SIDE].rearrange("p t h w -> p h w t"),
+                    )
 
-        def quantise_and_multiply(b, n, grouped):
-            codes = quantised.tile([P, POSITIONS], U32, align_bytes=64, name="codes")
-            scales = quantised.tile([P, POSITIONS], U8, align_bytes=64, name="scales")
-            nc.vector.quantize_mx(
-                out=codes[:].bitcast(FP8X4),
-                scales=scales[:],
-                in_=grouped[:].rearrange("p w t -> p (w t)"),
-            )
-            for half in range(halves):
-                columns = slice(half * N_TILE, (half + 1) * N_TILE)
-                nc.tensor.matmul_mx(
-                    out=acc[n][half][:],
-                    lhsT=w_words[:, b, :].bitcast(FP4X4),
-                    lhsT_scale=w_scales[:, b, :],
-                    rhs=codes[:, columns].bitcast(FP8X4),
-                    rhs_scale=scales[:, columns],
-                    start=(b == 0),
-                    stop=(b == PASSES - 1),
-                )
-            if b == PASSES - 1:
-                out_rows = out[n].rearrange("o p q -> o (p q)")
-                for half in range(halves):
+                    codes = quantised.tile([P, POSITIONS], U32, align_bytes=64)
+                    scales = quantised.tile([P, POSITIONS], U8, align_bytes=64)
+                    nc.vector.quantize_mx(
+                        out=codes[:].bitcast(FP8X4),
+                        scales=scales[:],
+                        in_=grouped[:].rearrange("p w t -> p (w t)"),
+                    )
+
+                    for g in range(QUARTERS):
+                        block = (GROUP_K * g + WORDS * PACK * z) // BLOCK_K
+                        for half in range(HALVES):
+                            columns = slice(half * N_TILE, (half + 1) * N_TILE)
+                            nc.tensor.matmul_mx(
+                                out=acc[i][half][:],
+                                lhsT=w_words[:, g, z, :].bitcast(FP4X4),
+                                lhsT_scale=w_scales[:, block, :],
+                                rhs=codes[:, columns].bitcast(FP8X4),
+                                rhs_scale=scales[:, columns],
+                                start=(z == 0 and g == 0),
+                                stop=(z == STEPS - 1 and g == QUARTERS - 1),
+                            )
+
+            for i in range(TOGETHER):
+                out_rows = out[first_image + i].rearrange("o p q -> o (p q)")
+                for half in range(HALVES):
                     columns = slice(half * N_TILE, (half + 1) * N_TILE)
-                    result = results.tile([OUT_CHANNELS, N_TILE], F32, name="result")
+                    result = results.tile([OUT_CHANNELS, N_TILE], F32)
                     nc.scalar.activation(
                         out=result[:],
-                        in_=acc[n][half][:],
+                        in_=acc[i][half][:],
                         func=mybir.ActivationFunctionType.Identity,
                         bias=bias_f32[:, 0:1],
                     )
-                    nc.sync.dma_start(out=out_rows[:, columns], in_=result[:])
-
-        assert IMAGES == PACK
-        with tc.manual_schedule():
-            for b in range(AHEAD):
-                raw_of_pass[b] = rows.tile([P, PACK, IMAGES, ROW_PITCH], BF16, name="raw")
-                for t in range(PACK):
-                    load_rows(b, t)
-                if b == 0:
-                    load_weight()
-            previous = None
-            for b in range(PASSES):
-                for n in range(IMAGES):
-                    if b + AHEAD < PASSES:
-                        if n == 0:
-                            raw_of_pass[b + AHEAD] = rows.tile([P, PACK, IMAGES, ROW_PITCH], BF16, name="raw")
-                        load_rows(b + AHEAD, n)
-                    current = (b, n, regroup(b, n))
-                    if previous is not None:
-                        quantise_and_multiply(*previous)
-                    previous = current
-            quantise_and_multiply(*previous)
+                    nc.scalar.dma_start(out=out_rows[:, columns], in_=result[:])

@@ -35,6 +35,7 @@ POSITIONS = OUT_SIDE * OUT_SIDE
 N_TILE = 512
 HALVES = POSITIONS // N_TILE
 TOGETHER = 2
+LOADS_AHEAD = 4
 
 VECTOR_ROWS = 18
 
@@ -51,11 +52,11 @@ def tile_sparseconv2d_kernel(tc, x, weight_words, weight_scales, bias, out):
     nc = tc.nc
     with (
         tc.tile_pool(name="keep", bufs=1) as keep,
-        tc.tile_pool(name="rows", bufs=4) as rows,
+        tc.tile_pool(name="rows", bufs=LOADS_AHEAD) as rows,
         tc.tile_pool(name="groups", bufs=4) as groups,
         tc.tile_pool(name="quantised", bufs=4) as quantised,
         tc.tile_pool(name="results", bufs=4) as results,
-        tc.psum_pool(name="sums", bufs=2) as sums,
+        tc.psum_pool(name="sums", bufs=1) as sums,
     ):
         w_words = keep.tile([P, QUARTERS, STEPS, 2 * OUT_CHANNELS], U8, align_bytes=64)
         nc.vector.memset(w_words[:].rearrange("p g z w -> p (g z w)").bitcast(I32), 0)
@@ -86,71 +87,94 @@ def tile_sparseconv2d_kernel(tc, x, weight_words, weight_scales, bias, out):
                         in_=word_rows[g, e],
                     )
             nc.sync.dma_start(out=bias_bf16[:], in_=bias)
-            nc.vector.tensor_copy(out=bias_f32[:], in_=bias_bf16[:])
+            nc.gpsimd.tensor_copy(out=bias_f32[:], in_=bias_bf16[:])
 
         x_groups = x.rearrange("n (u c) h w -> u n (c h w)", c=GROUP_CHANNELS)
+        acc = [
+            [sums.tile([OUT_CHANNELS, N_TILE], F32, name="acc%d_%d" % (n, half)) for half in range(HALVES)]
+            for n in range(IMAGES)
+        ]
+        loads = [(first_image, z) for first_image in range(0, IMAGES, TOGETHER) for z in range(STEPS)]
+        units = [(load, first_image + i, z) for load, (first_image, z) in enumerate(loads) for i in range(TOGETHER)]
+        raw_of_load = {}
+        grouped_of_unit = {}
 
-        for first_image in range(0, IMAGES, TOGETHER):
-            acc = [
-                [sums.tile([OUT_CHANNELS, N_TILE], F32, name="acc%d_%d" % (i, half)) for half in range(HALVES)]
-                for i in range(TOGETHER)
-            ]
-            for z in range(STEPS):
-                raw = rows.tile([P, PACK, TOGETHER, ROW_PITCH], BF16)
-                for t in range(PACK):
-                    for e in range(WORDS):
-                        start = row_start(WORDS * PACK * z + PACK * e + t)
-                        nc.sync.dma_start(
-                            out=raw[e:P:WORDS, t, :, 0:ROW],
-                            in_=x_groups[:, first_image : first_image + TOGETHER, start : start + ROW],
-                        )
-                if first_image == 0 and z == 0:
+        def load_rows(load):
+            first_image, z = loads[load]
+            raw_of_load[load] = rows.tile([P, PACK, TOGETHER, ROW_PITCH], BF16, name="raw")
+            for t in range(PACK):
+                for e in range(WORDS):
+                    start = row_start(WORDS * PACK * z + PACK * e + t)
+                    nc.sync.dma_start(
+                        out=raw_of_load[load][e:P:WORDS, t, :, 0:ROW],
+                        in_=x_groups[:, first_image : first_image + TOGETHER, start : start + ROW],
+                    )
+
+        def regroup(unit):
+            load, n, z = units[unit]
+            grouped = groups.tile([P, POSITIONS, PACK], BF16, align_bytes=64, name="grouped")
+            raw_rows = raw_of_load[load][:, :, n % TOGETHER, :]
+            raw_image = raw_rows.rearrange("p t (h w) -> p t h w", w=SIDE)[:, :, :, 0:OUT_SIDE]
+            grouped_image = grouped[:].rearrange("p (h w) t -> p h w t", w=OUT_SIDE)
+            nc.vector.tensor_copy(
+                out=grouped_image[:, 0:VECTOR_ROWS].rearrange("p h (c f) t -> p h c t f", f=PACK),
+                in_=raw_image[:, :, 0:VECTOR_ROWS].rearrange("p t h (c f) -> p h c t f", f=PACK),
+            )
+            nc.scalar.copy(
+                out=grouped_image[:, VECTOR_ROWS:OUT_SIDE],
+                in_=raw_image[:, :, VECTOR_ROWS:OUT_SIDE].rearrange("p t h w -> p h w t"),
+            )
+            grouped_of_unit[unit] = grouped
+
+        def quantise_and_multiply(unit):
+            load, n, z = units[unit]
+            codes = quantised.tile([P, POSITIONS], U32, align_bytes=64, name="codes")
+            scales = quantised.tile([P, POSITIONS], U8, align_bytes=64, name="scales")
+            nc.vector.quantize_mx(
+                out=codes[:].bitcast(FP8X4),
+                scales=scales[:],
+                in_=grouped_of_unit[unit][:].rearrange("p w t -> p (w t)"),
+            )
+            for half in range(HALVES):
+                columns = slice(half * N_TILE, (half + 1) * N_TILE)
+                for g in range(QUARTERS):
+                    block = (GROUP_K * g + WORDS * PACK * z) // BLOCK_K
+                    nc.tensor.matmul_mx(
+                        out=acc[n][half][:],
+                        lhsT=w_words[:, g, z, :].bitcast(FP4X4),
+                        lhsT_scale=w_scales[:, block, :],
+                        rhs=codes[:, columns].bitcast(FP8X4),
+                        rhs_scale=scales[:, columns],
+                        start=(z == 0 and g == 0),
+                        stop=(z == STEPS - 1 and g == QUARTERS - 1),
+                    )
+
+        def add_bias_and_store(n):
+            out_rows = out[n].rearrange("o p q -> o (p q)")
+            for half in range(HALVES):
+                columns = slice(half * N_TILE, (half + 1) * N_TILE)
+                result = results.tile([OUT_CHANNELS, N_TILE], F32, name="result")
+                nc.scalar.activation(
+                    out=result[:],
+                    in_=acc[n][half][:],
+                    func=mybir.ActivationFunctionType.Identity,
+                    bias=bias_f32[:, 0:1],
+                )
+                nc.scalar.dma_start(out=out_rows[:, columns], in_=result[:])
+
+        with tc.manual_schedule():
+            for load in range(LOADS_AHEAD):
+                load_rows(load)
+                if load == 1:
                     load_weight()
-
-                for i in range(TOGETHER):
-                    grouped = groups.tile([P, POSITIONS, PACK], BF16, align_bytes=64)
-                    raw_image = raw[:, :, i, :].rearrange("p t (h w) -> p t h w", w=SIDE)[:, :, :, 0:OUT_SIDE]
-                    grouped_image = grouped[:].rearrange("p (h w) t -> p h w t", w=OUT_SIDE)
-                    nc.vector.tensor_copy(
-                        out=grouped_image[:, 0:VECTOR_ROWS].rearrange("p h (c i) t -> p h c t i", i=PACK),
-                        in_=raw_image[:, :, 0:VECTOR_ROWS].rearrange("p t h (c i) -> p h c t i", i=PACK),
-                    )
-                    nc.scalar.copy(
-                        out=grouped_image[:, VECTOR_ROWS:OUT_SIDE],
-                        in_=raw_image[:, :, VECTOR_ROWS:OUT_SIDE].rearrange("p t h w -> p h w t"),
-                    )
-
-                    codes = quantised.tile([P, POSITIONS], U32, align_bytes=64)
-                    scales = quantised.tile([P, POSITIONS], U8, align_bytes=64)
-                    nc.vector.quantize_mx(
-                        out=codes[:].bitcast(FP8X4),
-                        scales=scales[:],
-                        in_=grouped[:].rearrange("p w t -> p (w t)"),
-                    )
-
-                    for g in range(QUARTERS):
-                        block = (GROUP_K * g + WORDS * PACK * z) // BLOCK_K
-                        for half in range(HALVES):
-                            columns = slice(half * N_TILE, (half + 1) * N_TILE)
-                            nc.tensor.matmul_mx(
-                                out=acc[i][half][:],
-                                lhsT=w_words[:, g, z, :].bitcast(FP4X4),
-                                lhsT_scale=w_scales[:, block, :],
-                                rhs=codes[:, columns].bitcast(FP8X4),
-                                rhs_scale=scales[:, columns],
-                                start=(z == 0 and g == 0),
-                                stop=(z == STEPS - 1 and g == QUARTERS - 1),
-                            )
-
-            for i in range(TOGETHER):
-                out_rows = out[first_image + i].rearrange("o p q -> o (p q)")
-                for half in range(HALVES):
-                    columns = slice(half * N_TILE, (half + 1) * N_TILE)
-                    result = results.tile([OUT_CHANNELS, N_TILE], F32)
-                    nc.scalar.activation(
-                        out=result[:],
-                        in_=acc[i][half][:],
-                        func=mybir.ActivationFunctionType.Identity,
-                        bias=bias_f32[:, 0:1],
-                    )
-                    nc.scalar.dma_start(out=out_rows[:, columns], in_=result[:])
+            for turn in range(len(units) + 2):
+                if turn < len(units):
+                    regroup(turn)
+                    load = units[turn][0]
+                    last_of_load = turn + 1 == len(units) or units[turn + 1][0] != load
+                    if last_of_load and load + LOADS_AHEAD < len(loads):
+                        load_rows(load + LOADS_AHEAD)
+                if 1 <= turn <= len(units):
+                    quantise_and_multiply(turn - 1)
+                if turn >= 2 and units[turn - 2][2] == STEPS - 1:
+                    add_bias_and_store(units[turn - 2][1])

@@ -34,8 +34,7 @@ ROW_PITCH = OUT_SIDE * SIDE
 POSITIONS = OUT_SIDE * OUT_SIDE
 N_TILE = 512
 HALVES = POSITIONS // N_TILE
-TOGETHER = 2
-LOADS_AHEAD = 4
+LOADS_AHEAD = 3
 
 VECTOR_ROWS = 18
 
@@ -94,26 +93,29 @@ def tile_sparseconv2d_kernel(tc, x, weight_words, weight_scales, bias, out):
             [sums.tile([OUT_CHANNELS, N_TILE], F32, name="acc%d_%d" % (n, half)) for half in range(HALVES)]
             for n in range(IMAGES)
         ]
-        loads = [(first_image, z) for first_image in range(0, IMAGES, TOGETHER) for z in range(STEPS)]
-        units = [(load, first_image + i, z) for load, (first_image, z) in enumerate(loads) for i in range(TOGETHER)]
+        loads = []
+        for z in range(STEPS):
+            images = IMAGES // 2 if z in (0, STEPS - 1) else IMAGES
+            loads.extend((first_image, images, z) for first_image in range(0, IMAGES, images))
+        units = [(load, first + i, z) for load, (first, images, z) in enumerate(loads) for i in range(images)]
         raw_of_load = {}
         grouped_of_unit = {}
 
         def load_rows(load):
-            first_image, z = loads[load]
-            raw_of_load[load] = rows.tile([P, PACK, TOGETHER, ROW_PITCH], BF16, name="raw")
+            first_image, images, z = loads[load]
+            raw_of_load[load] = rows.tile([P, PACK, images, ROW_PITCH], BF16, name="raw")
             for t in range(PACK):
                 for e in range(WORDS):
                     start = row_start(WORDS * PACK * z + PACK * e + t)
                     nc.sync.dma_start(
                         out=raw_of_load[load][e:P:WORDS, t, :, 0:ROW],
-                        in_=x_groups[:, first_image : first_image + TOGETHER, start : start + ROW],
+                        in_=x_groups[:, first_image : first_image + images, start : start + ROW],
                     )
 
         def regroup(unit):
             load, n, z = units[unit]
             grouped = groups.tile([P, POSITIONS, PACK], BF16, align_bytes=64, name="grouped")
-            raw_rows = raw_of_load[load][:, :, n % TOGETHER, :]
+            raw_rows = raw_of_load[load][:, :, n - loads[load][0], :]
             raw_image = raw_rows.rearrange("p t (h w) -> p t h w", w=SIDE)[:, :, :, 0:OUT_SIDE]
             grouped_image = grouped[:].rearrange("p (h w) t -> p h w t", w=OUT_SIDE)
             nc.vector.tensor_copy(

@@ -12,143 +12,201 @@ IMAGES = 4
 CHANNELS = 512
 SIDE = 34
 KERNEL = 3
-OUT_SIDE = SIDE - KERNEL + 1
+OUT_SIDE = 32
 OUT_CHANNELS = 128
-TAPS = KERNEL * KERNEL
+TAPS = 9
 PLANE = SIDE * SIDE
 
 P = 128
-PACK = 4
-WORDS = 2
-BLOCK_K = 32
-GROUP_CHANNELS = 8
-GROUP_K = GROUP_CHANNELS * TAPS
-GROUPS = CHANNELS // GROUP_CHANNELS
-STEPS = GROUP_K // (WORDS * PACK)
-QUARTERS = BLOCK_K // (WORDS * PACK)
-RUNS = GROUPS // QUARTERS
-RUN_BLOCKS = QUARTERS * GROUP_K // BLOCK_K
-
-ROW = (OUT_SIDE - 1) * SIDE + OUT_SIDE
-ROW_PITCH = OUT_SIDE * SIDE
-POSITIONS = OUT_SIDE * OUT_SIDE
+SETS = 3
+MASKS = 3
+KINDS = 3
+ROW = OUT_SIDE * SIDE
+PITCH = ROW + 16
+PAIR = 2 * PITCH
+SHIFT = 2
+TILE_IMAGES = (((0, 1), (2, 3)), ((0, 1, 2, 3),), ((0, 1, 2, 3),))
+POSITIONS = 1024
 N_TILE = 512
-HALVES = POSITIONS // N_TILE
-LOADS_AHEAD = 3
-
-VECTOR_ROWS = 18
+HALVES = 2
+HALF_ROWS = 16
+PAIRS = 16
 
 FLOPS = 2 * CHANNELS * TAPS * IMAGES * POSITIONS * OUT_CHANNELS
 
-
-def row_start(k_in_group):
-    channel, tap = divmod(k_in_group, TAPS)
-    kernel_row, kernel_column = divmod(tap, KERNEL)
-    return channel * PLANE + kernel_row * SIDE + kernel_column
+VECTOR_PIECES = (((0, 1), (0,), (0, 1)), ((0, 1), (0,), (0,)))
 
 
 def tile_sparseconv2d_kernel(tc, x, weight_words, weight_scales, bias, out):
     nc = tc.nc
     with (
         tc.tile_pool(name="keep", bufs=1) as keep,
-        tc.tile_pool(name="rows", bufs=LOADS_AHEAD) as rows,
         tc.tile_pool(name="groups", bufs=4) as groups,
-        tc.tile_pool(name="quantised", bufs=4) as quantised,
+        tc.tile_pool(name="quantised", bufs=6) as quantised,
         tc.tile_pool(name="results", bufs=4) as results,
         tc.psum_pool(name="sums", bufs=1) as sums,
     ):
-        w_words = keep.tile([P, QUARTERS, STEPS, 2 * OUT_CHANNELS], U8, align_bytes=64)
-        nc.vector.memset(w_words[:].rearrange("p g z w -> p (g z w)").bitcast(I32), 0)
-        w_scales = keep.tile([P, RUN_BLOCKS, OUT_CHANNELS], U8, align_bytes=64)
-        nc.vector.memset(w_scales[:].rearrange("p b o -> p (b o)").bitcast(I32), 0)
-
-        word_rows = (
-            weight_words.rearrange("a p w -> (a p) w")
-            .bitcast(I32)
-            .rearrange("(s g z e) w -> g e s z w", g=QUARTERS, z=STEPS, e=WORDS)
-        )
-        scale_rows = (
-            weight_scales.rearrange("a q o -> (a q) o").rearrange("(s b) o -> s (b o)", b=RUN_BLOCKS).bitcast(I32)
-        )
+        w_words = keep.tile([P, SETS, MASKS, KINDS + 1, 2 * OUT_CHANNELS], U8, align_bytes=64)
+        nc.vector.memset(w_words[:].rearrange("p z b w c -> p (z b w c)").bitcast(I32), 0)
+        w_scales = keep.tile([P, SETS, MASKS, OUT_CHANNELS], U8, align_bytes=64)
+        nc.vector.memset(w_scales[:].rearrange("p z b o -> p (z b o)").bitcast(I32), 0)
         bias_bf16 = keep.tile([P, 1], BF16)
         bias_f32 = keep.tile([P, 1], F32)
+
+        word_rows = weight_words.rearrange("a p c -> (a p) c").rearrange(
+            "(z g e w) c -> e g z (w c)", z=SETS, g=16, e=8, w=3
+        )
+        scale_rows = weight_scales.rearrange("a q o -> (a q) o").rearrange(
+            "(z g b) o -> g z (b o)", z=SETS, g=16, b=MASKS
+        )
 
         def load_weight():
             for quadrant in range(4):
                 nc.sync.dma_start(
-                    out=w_scales[32 * quadrant : 32 * quadrant + 4].rearrange("p b o -> p (b o)").bitcast(I32),
-                    in_=scale_rows[4 * quadrant : 4 * quadrant + 4, :],
+                    out=w_scales[32 * quadrant : 32 * quadrant + 4].rearrange("p z b o -> p z (b o)").bitcast(I32),
+                    in_=scale_rows[4 * quadrant : 4 * quadrant + 4].bitcast(I32),
                 )
-            for g in range(QUARTERS):
-                for e in range(WORDS):
-                    nc.sync.dma_start(
-                        out=w_words[WORDS * g + e : P : WORDS * QUARTERS, g, :, :].bitcast(I32),
-                        in_=word_rows[g, e],
-                    )
+            for e in range(8):
+                for block in range(MASKS):
+                    inside = [w for w in range(3) if (12 * e + 4 * w) // 32 == block]
+                    if inside:
+                        first, past = inside[0], inside[0] + len(inside)
+                        nc.sync.dma_start(
+                            out=w_words[e:P:8, :, block, first:past, :].rearrange("p z w c -> p z (w c)").bitcast(I32),
+                            in_=word_rows[e][:, :, 256 * first : 256 * past].bitcast(I32),
+                        )
             nc.sync.dma_start(out=bias_bf16[:], in_=bias)
             nc.gpsimd.tensor_copy(out=bias_f32[:], in_=bias_bf16[:])
 
-        x_groups = x.rearrange("n (u c) h w -> u n (c h w)", c=GROUP_CHANNELS)
+        def half_bytes(slot, odd):
+            return w_words[:, :, :, slot, :].rearrange("p z b (o two) -> p z b o two", two=2)[:, :, :, :, odd]
+
+        def move_bytes(to_slot, to_odd, from_slot, from_odd):
+            nc.vector.tensor_copy(out=half_bytes(to_slot, to_odd), in_=half_bytes(from_slot, from_odd))
+
+        x_quads = x.rearrange("n (v c) h w -> v n (c h w)", c=4)
+        raw_of_image = {}
+
+        def load_rows(z, members, queues):
+            region = len(members) * PAIR + 16
+            tile = keep.tile([P, 2 * region], BF16, name="raw%d_%d" % (z, members[0]))
+            for place, n in enumerate(members):
+                raw_of_image[(z, n)] = (tile, region, place)
+            for s in (0, 2, 1, 3):
+                u, g = divmod(s, 2)
+                first = g * (region + SHIFT)
+                view = tile[:, first : first + len(members) * PAIR].rearrange(
+                    "p (n u y) -> p n u y", n=len(members), u=2
+                )[:, :, u, 0:ROW]
+                for klass in range(3):
+                    p0 = (klass - P * z) % 3
+                    v0 = (P * z + p0 - klass) // 3
+                    channel, kernel_row = divmod(4 * klass + s, 3)
+                    start = channel * PLANE + kernel_row * SIDE
+                    count = len(range(p0, P, 3))
+                    for lo, hi in ((0, 32), (32, count)):
+                        queues[g].dma_start(
+                            out=view[p0 + 3 * lo : min(p0 + 3 * hi, P) : 3],
+                            in_=x_quads[v0 + lo : v0 + hi, members[0] : members[0] + len(members), start : start + ROW],
+                        )
+
         acc = [
             [sums.tile([OUT_CHANNELS, N_TILE], F32, name="acc%d_%d" % (n, half)) for half in range(HALVES)]
             for n in range(IMAGES)
         ]
-        loads = []
-        for z in range(STEPS):
-            images = IMAGES // 2 if z in (0, STEPS - 1) else IMAGES
-            loads.extend((first_image, images, z) for first_image in range(0, IMAGES, images))
-        units = [(load, first + i, z) for load, (first, images, z) in enumerate(loads) for i in range(images)]
-        raw_of_load = {}
+        units = [(z, kind, n) for z in range(SETS) for n in range(IMAGES) for kind in range(KINDS)]
         grouped_of_unit = {}
+        quantised_of_unit = {}
 
-        def load_rows(load):
-            first_image, images, z = loads[load]
-            raw_of_load[load] = rows.tile([P, PACK, images, ROW_PITCH], BF16, name="raw")
-            for t in range(PACK):
-                for e in range(WORDS):
-                    start = row_start(WORDS * PACK * z + PACK * e + t)
-                    nc.sync.dma_start(
-                        out=raw_of_load[load][e:P:WORDS, t, :, 0:ROW],
-                        in_=x_groups[:, first_image : first_image + images, start : start + ROW],
+        def pieces(unit, grouped):
+            z, kind, n = units[unit]
+            tile, region, place = raw_of_image[(z, n)]
+            found = []
+            out_words = grouped[:].bitcast(F32).rearrange(
+                "p (a r h q u) -> p a r h q u", a=HALVES, r=2, h=HALF_ROWS, q=PAIRS
+            )
+            out_values = grouped[:].rearrange(
+                "p (a r h q u t) -> p a r h q u t", a=HALVES, r=2, h=HALF_ROWS, q=PAIRS, u=2
+            )
+            if kind < 2:
+                base = kind * (region + SHIFT) + place * PAIR
+                words = (
+                    tile[:, base : base + PAIR]
+                    .bitcast(F32)
+                    .rearrange("p (u y) -> p u y", u=2)[:, :, 0 : ROW // 2]
+                    .rearrange("p u (h w) -> p u h w", w=SIDE // 2)
+                )
+                values = (
+                    tile[:, base : base + PAIR]
+                    .rearrange("p (u y) -> p u y", u=2)[:, :, 1 : 1 + ROW]
+                    .rearrange("p u (h w t) -> p u h w t", w=SIDE // 2, t=2)
+                )
+                found.append(
+                    (
+                        out_words[:, :, kind],
+                        words[:, :, :, kind : kind + PAIRS].rearrange("p u (a h) q -> p a h q u", a=HALVES),
                     )
+                )
+                for a in range(HALVES):
+                    found.append(
+                        (
+                            out_values[:, a, 1 - kind],
+                            values[:, :, HALF_ROWS * a : HALF_ROWS * (a + 1), 0:PAIRS, :].rearrange(
+                                "p u h q t -> p h q u t"
+                            ),
+                        )
+                    )
+            else:
+                base = SHIFT + place * PAIR
+                values = (
+                    tile[:]
+                    .rearrange("p (t y) -> p t y", t=2)[:, :, base : base + PAIR]
+                    .rearrange("p t (u y) -> p t u y", u=2)[:, :, :, 0:ROW]
+                    .rearrange("p t u (h w r) -> p t u h w r", w=SIDE // 2, r=2)
+                )
+                for a in range(HALVES):
+                    for r in range(2):
+                        found.append(
+                            (
+                                out_values[:, a, r],
+                                values[:, :, :, HALF_ROWS * a : HALF_ROWS * (a + 1), 0:PAIRS, r].rearrange(
+                                    "p t u h q -> p h q u t"
+                                ),
+                            )
+                        )
+            return found
 
         def regroup(unit):
-            load, n, z = units[unit]
-            grouped = groups.tile([P, POSITIONS, PACK], BF16, align_bytes=64, name="grouped")
-            raw_rows = raw_of_load[load][:, :, n - loads[load][0], :]
-            raw_image = raw_rows.rearrange("p t (h w) -> p t h w", w=SIDE)[:, :, :, 0:OUT_SIDE]
-            grouped_image = grouped[:].rearrange("p (h w) t -> p h w t", w=OUT_SIDE)
-            nc.vector.tensor_copy(
-                out=grouped_image[:, 0:VECTOR_ROWS].rearrange("p h (c f) t -> p h c t f", f=PACK),
-                in_=raw_image[:, :, 0:VECTOR_ROWS].rearrange("p t h (c f) -> p h c t f", f=PACK),
-            )
-            nc.scalar.copy(
-                out=grouped_image[:, VECTOR_ROWS:OUT_SIDE],
-                in_=raw_image[:, :, VECTOR_ROWS:OUT_SIDE].rearrange("p t h w -> p h w t"),
-            )
+            z, kind, n = units[unit]
+            grouped = groups.tile([P, 4 * POSITIONS], BF16, align_bytes=64, name="grouped")
+            for number, (to, source) in enumerate(pieces(unit, grouped)):
+                if number in VECTOR_PIECES[n % 2][kind]:
+                    nc.vector.tensor_copy(out=to, in_=source)
+                else:
+                    nc.scalar.copy(out=to, in_=source)
             grouped_of_unit[unit] = grouped
 
-        def quantise_and_multiply(unit):
-            load, n, z = units[unit]
+        def quantise(unit):
             codes = quantised.tile([P, POSITIONS], U32, align_bytes=64, name="codes")
             scales = quantised.tile([P, POSITIONS], U8, align_bytes=64, name="scales")
-            nc.vector.quantize_mx(
-                out=codes[:].bitcast(FP8X4),
-                scales=scales[:],
-                in_=grouped_of_unit[unit][:].rearrange("p w t -> p (w t)"),
-            )
+            nc.vector.quantize_mx(out=codes[:].bitcast(FP8X4), scales=scales[:], in_=grouped_of_unit[unit][:])
+            quantised_of_unit[unit] = (codes, scales)
+
+        def multiply(unit):
+            z, kind, n = units[unit]
+            codes, scales = quantised_of_unit[unit]
+            slot = (0, 1, 3)[kind]
             for half in range(HALVES):
                 columns = slice(half * N_TILE, (half + 1) * N_TILE)
-                for g in range(QUARTERS):
-                    block = (GROUP_K * g + WORDS * PACK * z) // BLOCK_K
+                for block in range(MASKS):
                     nc.tensor.matmul_mx(
                         out=acc[n][half][:],
-                        lhsT=w_words[:, g, z, :].bitcast(FP4X4),
-                        lhsT_scale=w_scales[:, block, :],
+                        lhsT=w_words[:, z, block, slot, :].bitcast(FP4X4),
+                        lhsT_scale=w_scales[:, z, block, :],
                         rhs=codes[:, columns].bitcast(FP8X4),
                         rhs_scale=scales[:, columns],
-                        start=(z == 0 and g == 0),
-                        stop=(z == STEPS - 1 and g == QUARTERS - 1),
+                        start=(z == 0 and kind == 0 and block == 0),
+                        stop=(z == SETS - 1 and kind == KINDS - 1 and block == MASKS - 1),
                     )
 
         def add_bias_and_store(n):
@@ -157,26 +215,32 @@ def tile_sparseconv2d_kernel(tc, x, weight_words, weight_scales, bias, out):
                 columns = slice(half * N_TILE, (half + 1) * N_TILE)
                 result = results.tile([OUT_CHANNELS, N_TILE], F32, name="result")
                 nc.scalar.activation(
-                    out=result[:],
-                    in_=acc[n][half][:],
+                    out=result[:].rearrange("o (m r) -> o m r", r=2),
+                    in_=acc[n][half][:].rearrange("o (r m) -> o m r", r=2),
                     func=mybir.ActivationFunctionType.Identity,
                     bias=bias_f32[:, 0:1],
                 )
                 nc.scalar.dma_start(out=out_rows[:, columns], in_=result[:])
 
         with tc.manual_schedule():
-            for load in range(LOADS_AHEAD):
-                load_rows(load)
-                if load == 1:
-                    load_weight()
-            for turn in range(len(units) + 2):
+            for z in range(SETS):
+                for members in TILE_IMAGES[z]:
+                    if z == 0 and members[0] == 0:
+                        load_rows(z, members, (nc.sync, nc.scalar))
+                        load_weight()
+                    else:
+                        load_rows(z, members, (nc.sync, nc.sync))
+            for turn in range(len(units) + 3):
                 if turn < len(units):
                     regroup(turn)
-                    load = units[turn][0]
-                    last_of_load = turn + 1 == len(units) or units[turn + 1][0] != load
-                    if last_of_load and load + LOADS_AHEAD < len(loads):
-                        load_rows(load + LOADS_AHEAD)
                 if 1 <= turn <= len(units):
-                    quantise_and_multiply(turn - 1)
-                if turn >= 2 and units[turn - 2][2] == STEPS - 1:
-                    add_bias_and_store(units[turn - 2][1])
+                    quantise(turn - 1)
+                if turn == 2:
+                    move_bytes(3, 0, 0, 1)
+                    move_bytes(0, 1, 1, 1)
+                    move_bytes(3, 1, 2, 0)
+                    move_bytes(1, 1, 2, 1)
+                if 2 <= turn <= len(units) + 1:
+                    multiply(turn - 2)
+                if turn >= 3 and units[turn - 3][0] == SETS - 1 and units[turn - 3][1] == KINDS - 1:
+                    add_bias_and_store(units[turn - 3][2])

@@ -34,7 +34,7 @@ PAIRS = 16
 
 FLOPS = 2 * CHANNELS * TAPS * IMAGES * POSITIONS * OUT_CHANNELS
 
-VECTOR_PIECES = (((0, 1), (0,), (0, 1)), ((0, 1), (0,), (0,)))
+VECTOR_PIECES = (((0, 1), (0, 1), (0, 1)), ((0, 1), (0, 1), (0, 1)))
 
 
 def tile_sparseconv2d_kernel(tc, x, weight_words, weight_scales, bias, out):

@@ -34,7 +34,7 @@ PAIRS = 16
 
 FLOPS = 2 * CHANNELS * TAPS * IMAGES * POSITIONS * OUT_CHANNELS
 
-VECTOR_PIECES = (((0, 1), (0, 1), (0, 1)), ((0, 1), (0, 1), (0, 1)))
+VECTOR_PIECES = (((0, 1), (0,), (0,)), ((0,), (1,), (0,)))
 
 
 def tile_sparseconv2d_kernel(tc, x, weight_words, weight_scales, bias, out):
@@ -147,15 +147,12 @@ def tile_sparseconv2d_kernel(tc, x, weight_words, weight_scales, bias, out):
                         words[:, :, :, kind : kind + PAIRS].rearrange("p u (a h) q -> p a h q u", a=HALVES),
                     )
                 )
-                for a in range(HALVES):
-                    found.append(
-                        (
-                            out_values[:, a, 1 - kind],
-                            values[:, :, HALF_ROWS * a : HALF_ROWS * (a + 1), 0:PAIRS, :].rearrange(
-                                "p u h q t -> p h q u t"
-                            ),
-                        )
+                found.append(
+                    (
+                        out_values[:, :, 1 - kind],
+                        values[:, :, :, 0:PAIRS, :].rearrange("p u (a h) q t -> p a h q u t", a=HALVES),
                     )
+                )
             else:
                 base = SHIFT + place * PAIR
                 values = (
@@ -164,16 +161,13 @@ def tile_sparseconv2d_kernel(tc, x, weight_words, weight_scales, bias, out):
                     .rearrange("p t (u y) -> p t u y", u=2)[:, :, :, 0:ROW]
                     .rearrange("p t u (h w r) -> p t u h w r", w=SIDE // 2, r=2)
                 )
-                for a in range(HALVES):
-                    for r in range(2):
-                        found.append(
-                            (
-                                out_values[:, a, r],
-                                values[:, :, :, HALF_ROWS * a : HALF_ROWS * (a + 1), 0:PAIRS, r].rearrange(
-                                    "p t u h q -> p h q u t"
-                                ),
-                            )
+                for r in range(2):
+                    found.append(
+                        (
+                            out_values[:, :, r],
+                            values[:, :, :, :, 0:PAIRS, r].rearrange("p t u (a h) q -> p a h q u t", a=HALVES),
                         )
+                    )
             return found
 
         def regroup(unit):

@@ -34,7 +34,7 @@ PAIRS = 16
 
 FLOPS = 2 * CHANNELS * TAPS * IMAGES * POSITIONS * OUT_CHANNELS
 
-VECTOR_PIECES = (((0, 1), (0,), (0,)), ((0,), (1,), (0,)))
+VECTOR_ROWS = (0, 16, 16)
 
 
 def tile_sparseconv2d_kernel(tc, x, weight_words, weight_scales, bias, out):
@@ -122,12 +122,8 @@ def tile_sparseconv2d_kernel(tc, x, weight_words, weight_scales, bias, out):
             z, kind, n = units[unit]
             tile, region, place = raw_of_image[(z, n)]
             found = []
-            out_words = grouped[:].bitcast(F32).rearrange(
-                "p (a r h q u) -> p a r h q u", a=HALVES, r=2, h=HALF_ROWS, q=PAIRS
-            )
-            out_values = grouped[:].rearrange(
-                "p (a r h q u t) -> p a r h q u t", a=HALVES, r=2, h=HALF_ROWS, q=PAIRS, u=2
-            )
+            out_words = grouped[:].bitcast(F32).rearrange("p (h r q u) -> p h r q u", h=OUT_SIDE, r=2, q=PAIRS)
+            out_values = grouped[:].rearrange("p (h r q u t) -> p h r q u t", h=OUT_SIDE, r=2, q=PAIRS, u=2)
             if kind < 2:
                 base = kind * (region + SHIFT) + place * PAIR
                 words = (
@@ -143,16 +139,20 @@ def tile_sparseconv2d_kernel(tc, x, weight_words, weight_scales, bias, out):
                 )
                 found.append(
                     (
+                        nc.vector,
                         out_words[:, :, kind],
-                        words[:, :, :, kind : kind + PAIRS].rearrange("p u (a h) q -> p a h q u", a=HALVES),
+                        words[:, :, :, kind : kind + PAIRS].rearrange("p u h q -> p h q u"),
                     )
                 )
-                found.append(
-                    (
-                        out_values[:, :, 1 - kind],
-                        values[:, :, :, 0:PAIRS, :].rearrange("p u (a h) q t -> p a h q u t", a=HALVES),
-                    )
-                )
+                for engine, low, high in ((nc.vector, 0, VECTOR_ROWS[kind]), (nc.scalar, VECTOR_ROWS[kind], OUT_SIDE)):
+                    if high > low:
+                        found.append(
+                            (
+                                engine,
+                                out_values[:, low:high, 1 - kind],
+                                values[:, :, low:high, 0:PAIRS, :].rearrange("p u h q t -> p h q u t"),
+                            )
+                        )
             else:
                 base = SHIFT + place * PAIR
                 values = (
@@ -161,20 +161,21 @@ def tile_sparseconv2d_kernel(tc, x, weight_words, weight_scales, bias, out):
                     .rearrange("p t (u y) -> p t u y", u=2)[:, :, :, 0:ROW]
                     .rearrange("p t u (h w r) -> p t u h w r", w=SIDE // 2, r=2)
                 )
-                for r in range(2):
-                    found.append(
-                        (
-                            out_values[:, :, r],
-                            values[:, :, :, :, 0:PAIRS, r].rearrange("p t u (a h) q -> p a h q u t", a=HALVES),
+                for engine, low, high in ((nc.vector, 0, VECTOR_ROWS[kind]), (nc.scalar, VECTOR_ROWS[kind], OUT_SIDE)):
+                    if high > low:
+                        found.append(
+                            (
+                                engine,
+                                out_values[:, low:high].rearrange("p h r q u t -> p h q r u t"),
+                                values[:, :, :, low:high, 0:PAIRS, :].rearrange("p t u h q r -> p h q r u t"),
+                            )
                         )
-                    )
             return found
 
         def regroup(unit):
-            z, kind, n = units[unit]
             grouped = groups.tile([P, 4 * POSITIONS], BF16, align_bytes=64, name="grouped")
-            for number, (to, source) in enumerate(pieces(unit, grouped)):
-                if number in VECTOR_PIECES[n % 2][kind]:
+            for engine, to, source in pieces(unit, grouped):
+                if engine is nc.vector:
                     nc.vector.tensor_copy(out=to, in_=source)
                 else:
                     nc.scalar.copy(out=to, in_=source)
@@ -209,8 +210,8 @@ def tile_sparseconv2d_kernel(tc, x, weight_words, weight_scales, bias, out):
                 columns = slice(half * N_TILE, (half + 1) * N_TILE)
                 result = results.tile([OUT_CHANNELS, N_TILE], F32, name="result")
                 nc.scalar.activation(
-                    out=result[:].rearrange("o (m r) -> o m r", r=2),
-                    in_=acc[n][half][:].rearrange("o (r m) -> o m r", r=2),
+                    out=result[:].rearrange("o (h q r) -> o h q r", h=HALF_ROWS, r=2),
+                    in_=acc[n][half][:].rearrange("o (h r q) -> o h q r", h=HALF_ROWS, r=2),
                     func=mybir.ActivationFunctionType.Identity,
                     bias=bias_f32[:, 0:1],
                 )

@@ -25,7 +25,8 @@ ROW = OUT_SIDE * SIDE
 PITCH = ROW + 16
 PAIR = 2 * PITCH
 SHIFT = 2
-TILE_IMAGES = (((0, 1), (2, 3)), ((0, 1, 2, 3),), ((0, 1, 2, 3),))
+TILE_IMAGES = (((0, 1, 2, 3),), ((0, 1, 2, 3),), ((0, 1, 2, 3),))
+THIRD = 42
 POSITIONS = 1024
 N_TILE = 512
 HALVES = 2
@@ -85,6 +86,7 @@ def tile_sparseconv2d_kernel(tc, x, weight_words, weight_scales, bias, out):
             nc.vector.tensor_copy(out=half_bytes(to_slot, to_odd), in_=half_bytes(from_slot, from_odd))
 
         x_quads = x.rearrange("n (v c) h w -> v n (c h w)", c=4)
+        x_flat = x.rearrange("n c h w -> n (c h w)")
         raw_of_image = {}
 
         def load_rows(z, members, queues):
@@ -98,17 +100,27 @@ def tile_sparseconv2d_kernel(tc, x, weight_words, weight_scales, bias, out):
                 view = tile[:, first : first + len(members) * PAIR].rearrange(
                     "p (n u y) -> p n u y", n=len(members), u=2
                 )[:, :, u, 0:ROW]
+                images = slice(members[0], members[0] + len(members))
                 for klass in range(3):
                     p0 = (klass - P * z) % 3
                     v0 = (P * z + p0 - klass) // 3
                     channel, kernel_row = divmod(4 * klass + s, 3)
                     start = channel * PLANE + kernel_row * SIDE
-                    count = len(range(p0, P, 3))
-                    for lo, hi in ((0, 32), (32, count)):
-                        queues[g].dma_start(
-                            out=view[p0 + 3 * lo : min(p0 + 3 * hi, P) : 3],
-                            in_=x_quads[v0 + lo : v0 + hi, members[0] : members[0] + len(members), start : start + ROW],
-                        )
+                    queues[g].dma_start(
+                        out=view[p0 : 3 * THIRD : 3], in_=x_quads[v0 : v0 + THIRD, images, start : start + ROW]
+                    )
+                starts = []
+                for p in (3 * THIRD, 3 * THIRD + 1):
+                    channel, kernel_row = divmod(4 * (P * z + p) + s, 3)
+                    starts.append(channel * PLANE + kernel_row * SIDE)
+                step = starts[1] - starts[0]
+                back = max(0, starts[0] + 2 * step - CHANNELS * PLANE)
+                queues[g].dma_start(
+                    out=view[3 * THIRD : P],
+                    in_=x_flat[images, starts[0] - back : starts[0] - back + 2 * step].rearrange(
+                        "n (l y) -> l n y", l=2
+                    )[:, :, back : back + ROW],
+                )
 
         acc = [
             [sums.tile([OUT_CHANNELS, N_TILE], F32, name="acc%d_%d" % (n, half)) for half in range(HALVES)]
@@ -221,7 +233,7 @@ def tile_sparseconv2d_kernel(tc, x, weight_words, weight_scales, bias, out):
             for z in range(SETS):
                 for members in TILE_IMAGES[z]:
                     if z == 0 and members[0] == 0:
-                        load_rows(z, members, (nc.sync, nc.scalar))
+                        load_rows(z, members, (nc.sync, nc.sync))
                         load_weight()
                     else:
                         load_rows(z, members, (nc.sync, nc.sync))

@@ -35,14 +35,14 @@ PAIRS = 16
 
 FLOPS = 2 * CHANNELS * TAPS * IMAGES * POSITIONS * OUT_CHANNELS
 
-VECTOR_ROWS = (0, 16, 16)
+VECTOR_ROWS = (32, 32, 0)
 
 
 def tile_sparseconv2d_kernel(tc, x, weight_words, weight_scales, bias, out):
     nc = tc.nc
     with (
         tc.tile_pool(name="keep", bufs=1) as keep,
-        tc.tile_pool(name="groups", bufs=4) as groups,
+        tc.tile_pool(name="groups", bufs=6) as groups,
         tc.tile_pool(name="quantised", bufs=6) as quantised,
         tc.tile_pool(name="results", bufs=4) as results,
         tc.psum_pool(name="sums", bufs=1) as sums,

@@ -25,7 +25,7 @@ ROW = OUT_SIDE * SIDE
 PITCH = ROW + 16
 PAIR = 2 * PITCH
 SHIFT = 2
-TILE_IMAGES = (((0, 1, 2, 3),), ((0, 1, 2, 3),), ((0, 1, 2, 3),))
+TILE_IMAGES = (((0, 1), (2, 3)), ((0, 1, 2, 3),), ((0, 1, 2, 3),))
 THIRD = 42
 POSITIONS = 1024
 N_TILE = 512
@@ -35,7 +35,7 @@ PAIRS = 16
 
 FLOPS = 2 * CHANNELS * TAPS * IMAGES * POSITIONS * OUT_CHANNELS
 
-VECTOR_ROWS = (32, 32, 0)
+VECTOR_ROWS = (32, 22, 0)
 
 
 def tile_sparseconv2d_kernel(tc, x, weight_words, weight_scales, bias, out):
@@ -89,12 +89,14 @@ def tile_sparseconv2d_kernel(tc, x, weight_words, weight_scales, bias, out):
         x_flat = x.rearrange("n c h w -> n (c h w)")
         raw_of_image = {}
 
-        def load_rows(z, members, queues):
+        def load_rows(z, members, queues, halfway=None):
             region = len(members) * PAIR + 16
             tile = keep.tile([P, 2 * region], BF16, name="raw%d_%d" % (z, members[0]))
             for place, n in enumerate(members):
                 raw_of_image[(z, n)] = (tile, region, place)
             for s in (0, 2, 1, 3):
+                if s == 1 and halfway is not None:
+                    halfway()
                 u, g = divmod(s, 2)
                 first = g * (region + SHIFT)
                 view = tile[:, first : first + len(members) * PAIR].rearrange(
@@ -194,24 +196,32 @@ def tile_sparseconv2d_kernel(tc, x, weight_words, weight_scales, bias, out):
             grouped_of_unit[unit] = grouped
 
         def quantise(unit):
-            codes = quantised.tile([P, POSITIONS], U32, align_bytes=64, name="codes")
-            scales = quantised.tile([P, POSITIONS], U8, align_bytes=64, name="scales")
-            nc.vector.quantize_mx(out=codes[:].bitcast(FP8X4), scales=scales[:], in_=grouped_of_unit[unit][:])
-            quantised_of_unit[unit] = (codes, scales)
+            calls = HALVES if unit == len(units) - 1 else 1
+            width = POSITIONS // calls
+            quantised_of_unit[unit] = []
+            for call in range(calls):
+                codes = quantised.tile([P, width], U32, align_bytes=64, name="codes")
+                scales = quantised.tile([P, width], U8, align_bytes=64, name="scales")
+                nc.vector.quantize_mx(
+                    out=codes[:].bitcast(FP8X4),
+                    scales=scales[:],
+                    in_=grouped_of_unit[unit][:, 4 * width * call : 4 * width * (call + 1)],
+                )
+                for first in range(0, width, N_TILE):
+                    quantised_of_unit[unit].append((codes[:, first : first + N_TILE], scales[:, first : first + N_TILE]))
 
         def multiply(unit):
             z, kind, n = units[unit]
-            codes, scales = quantised_of_unit[unit]
             slot = (0, 1, 3)[kind]
             for half in range(HALVES):
-                columns = slice(half * N_TILE, (half + 1) * N_TILE)
+                codes, scales = quantised_of_unit[unit][half]
                 for block in range(MASKS):
                     nc.tensor.matmul_mx(
                         out=acc[n][half][:],
                         lhsT=w_words[:, z, block, slot, :].bitcast(FP4X4),
                         lhsT_scale=w_scales[:, z, block, :],
-                        rhs=codes[:, columns].bitcast(FP8X4),
-                        rhs_scale=scales[:, columns],
+                        rhs=codes.bitcast(FP8X4),
+                        rhs_scale=scales,
                         start=(z == 0 and kind == 0 and block == 0),
                         stop=(z == SETS - 1 and kind == KINDS - 1 and block == MASKS - 1),
                     )
@@ -229,11 +239,16 @@ def tile_sparseconv2d_kernel(tc, x, weight_words, weight_scales, bias, out):
                 )
                 nc.scalar.dma_start(out=out_rows[:, columns], in_=result[:])
 
+        moves_before_unit = {
+            0: ((3, 0, 0, 1), (0, 1, 1, 1)),
+            1: ((1, 1, 2, 1),),
+            2: ((3, 1, 2, 0),),
+        }
         with tc.manual_schedule():
             for z in range(SETS):
                 for members in TILE_IMAGES[z]:
                     if z == 0 and members[0] == 0:
-                        load_rows(z, members, (nc.sync, nc.sync))
+                        load_rows(z, members, (nc.sync, nc.scalar))
                         load_weight()
                     else:
                         load_rows(z, members, (nc.sync, nc.sync))
@@ -242,12 +257,8 @@ def tile_sparseconv2d_kernel(tc, x, weight_words, weight_scales, bias, out):
                     regroup(turn)
                 if 1 <= turn <= len(units):
                     quantise(turn - 1)
-                if turn == 2:
-                    move_bytes(3, 0, 0, 1)
-                    move_bytes(0, 1, 1, 1)
-                    move_bytes(3, 1, 2, 0)
-                    move_bytes(1, 1, 2, 1)
-                if 2 <= turn <= len(units) + 1:
-                    multiply(turn - 2)
+                    for move in moves_before_unit.get(turn - 1, ()):
+                        move_bytes(move[0], move[1], move[2], move[3])
+                    multiply(turn - 1)
                 if turn >= 3 and units[turn - 3][0] == SETS - 1 and units[turn - 3][1] == KINDS - 1:
                     add_bias_and_store(units[turn - 3][2])

@@ -25,7 +25,7 @@ ROW = OUT_SIDE * SIDE
 PITCH = ROW + 16
 PAIR = 2 * PITCH
 SHIFT = 2
-TILE_IMAGES = (((0, 1), (2, 3)), ((0, 1, 2, 3),), ((0, 1, 2, 3),))
+TILE_IMAGES = (((0, 1), (2, 3)), ((0, 1), (2, 3)), ((0, 1), (2, 3)))
 THIRD = 42
 POSITIONS = 1024
 N_TILE = 512

import concourse.mybir as mybir

BF16 = mybir.dt.bfloat16
F32 = mybir.dt.float32
I32 = mybir.dt.int32
U8 = mybir.dt.uint8
U32 = mybir.dt.uint32
FP8X4 = mybir.dt.float8_e4m3fn_x4
FP4X4 = mybir.dt.float4_e2m1fn_x4

IMAGES = 4
CHANNELS = 512
SIDE = 34
KERNEL = 3
OUT_SIDE = 32
OUT_CHANNELS = 128
TAPS = 9
PLANE = SIDE * SIDE

P = 128
SETS = 3
MASKS = 3
KINDS = 3
ROW = OUT_SIDE * SIDE
PITCH = ROW + 16
PAIR = 2 * PITCH
SHIFT = 2
TILE_IMAGES = (((0, 1), (2, 3)), ((0, 1), (2, 3)), ((0, 1), (2, 3)))
THIRD = 42
POSITIONS = 1024
N_TILE = 512
HALVES = 2
HALF_ROWS = 16
PAIRS = 16

FLOPS = 2 * CHANNELS * TAPS * IMAGES * POSITIONS * OUT_CHANNELS

VECTOR_ROWS = (32, 22, 0)


def tile_sparseconv2d_kernel(tc, x, weight_words, weight_scales, bias, out):
    nc = tc.nc
    with (
        tc.tile_pool(name="keep", bufs=1) as keep,
        tc.tile_pool(name="groups", bufs=6) as groups,
        tc.tile_pool(name="quantised", bufs=6) as quantised,
        tc.tile_pool(name="results", bufs=4) as results,
        tc.psum_pool(name="sums", bufs=1) as sums,
    ):
        w_words = keep.tile([P, SETS, MASKS, KINDS + 1, 2 * OUT_CHANNELS], U8, align_bytes=64)
        nc.vector.memset(w_words[:].rearrange("p z b w c -> p (z b w c)").bitcast(I32), 0)
        w_scales = keep.tile([P, SETS, MASKS, OUT_CHANNELS], U8, align_bytes=64)
        nc.vector.memset(w_scales[:].rearrange("p z b o -> p (z b o)").bitcast(I32), 0)
        bias_bf16 = keep.tile([P, 1], BF16)
        bias_f32 = keep.tile([P, 1], F32)

        word_rows = weight_words.rearrange("a p c -> (a p) c").rearrange(
            "(z g e w) c -> e g z (w c)", z=SETS, g=16, e=8, w=3
        )
        scale_rows = weight_scales.rearrange("a q o -> (a q) o").rearrange(
            "(z g b) o -> g z (b o)", z=SETS, g=16, b=MASKS
        )

        def load_weight():
            for quadrant in range(4):
                nc.sync.dma_start(
                    out=w_scales[32 * quadrant : 32 * quadrant + 4].rearrange("p z b o -> p z (b o)").bitcast(I32),
                    in_=scale_rows[4 * quadrant : 4 * quadrant + 4].bitcast(I32),
                )
            for e in range(8):
                for block in range(MASKS):
                    inside = [w for w in range(3) if (12 * e + 4 * w) // 32 == block]
                    if inside:
                        first, past = inside[0], inside[0] + len(inside)
                        nc.sync.dma_start(
                            out=w_words[e:P:8, :, block, first:past, :].rearrange("p z w c -> p z (w c)").bitcast(I32),
                            in_=word_rows[e][:, :, 256 * first : 256 * past].bitcast(I32),
                        )
            nc.sync.dma_start(out=bias_bf16[:], in_=bias)
            nc.gpsimd.tensor_copy(out=bias_f32[:], in_=bias_bf16[:])

        def half_bytes(slot, odd):
            return w_words[:, :, :, slot, :].rearrange("p z b (o two) -> p z b o two", two=2)[:, :, :, :, odd]

        def move_bytes(to_slot, to_odd, from_slot, from_odd):
            nc.vector.tensor_copy(out=half_bytes(to_slot, to_odd), in_=half_bytes(from_slot, from_odd))

        x_quads = x.rearrange("n (v c) h w -> v n (c h w)", c=4)
        x_flat = x.rearrange("n c h w -> n (c h w)")
        raw_of_image = {}

        def load_rows(z, members, queues, halfway=None):
            region = len(members) * PAIR + 16
            tile = keep.tile([P, 2 * region], BF16, name="raw%d_%d" % (z, members[0]))
            for place, n in enumerate(members):
                raw_of_image[(z, n)] = (tile, region, place)
            for s in (0, 2, 1, 3):
                if s == 1 and halfway is not None:
                    halfway()
                u, g = divmod(s, 2)
                first = g * (region + SHIFT)
                view = tile[:, first : first + len(members) * PAIR].rearrange(
                    "p (n u y) -> p n u y", n=len(members), u=2
                )[:, :, u, 0:ROW]
                images = slice(members[0], members[0] + len(members))
                for klass in range(3):
                    p0 = (klass - P * z) % 3
                    v0 = (P * z + p0 - klass) // 3
                    channel, kernel_row = divmod(4 * klass + s, 3)
                    start = channel * PLANE + kernel_row * SIDE
                    queues[g].dma_start(
                        out=view[p0 : 3 * THIRD : 3], in_=x_quads[v0 : v0 + THIRD, images, start : start + ROW]
                    )
                starts = []
                for p in (3 * THIRD, 3 * THIRD + 1):
                    channel, kernel_row = divmod(4 * (P * z + p) + s, 3)
                    starts.append(channel * PLANE + kernel_row * SIDE)
                step = starts[1] - starts[0]
                back = max(0, starts[0] + 2 * step - CHANNELS * PLANE)
                queues[g].dma_start(
                    out=view[3 * THIRD : P],
                    in_=x_flat[images, starts[0] - back : starts[0] - back + 2 * step].rearrange(
                        "n (l y) -> l n y", l=2
                    )[:, :, back : back + ROW],
                )

        acc = [
            [sums.tile([OUT_CHANNELS, N_TILE], F32, name="acc%d_%d" % (n, half)) for half in range(HALVES)]
            for n in range(IMAGES)
        ]
        units = [(z, kind, n) for z in range(SETS) for n in range(IMAGES) for kind in range(KINDS)]
        grouped_of_unit = {}
        quantised_of_unit = {}

        def pieces(unit, grouped):
            z, kind, n = units[unit]
            tile, region, place = raw_of_image[(z, n)]
            found = []
            out_words = grouped[:].bitcast(F32).rearrange("p (h r q u) -> p h r q u", h=OUT_SIDE, r=2, q=PAIRS)
            out_values = grouped[:].rearrange("p (h r q u t) -> p h r q u t", h=OUT_SIDE, r=2, q=PAIRS, u=2)
            if kind < 2:
                base = kind * (region + SHIFT) + place * PAIR
                words = (
                    tile[:, base : base + PAIR]
                    .bitcast(F32)
                    .rearrange("p (u y) -> p u y", u=2)[:, :, 0 : ROW // 2]
                    .rearrange("p u (h w) -> p u h w", w=SIDE // 2)
                )
                values = (
                    tile[:, base : base + PAIR]
                    .rearrange("p (u y) -> p u y", u=2)[:, :, 1 : 1 + ROW]
                    .rearrange("p u (h w t) -> p u h w t", w=SIDE // 2, t=2)
                )
                found.append(
                    (
                        nc.vector,
                        out_words[:, :, kind],
                        words[:, :, :, kind : kind + PAIRS].rearrange("p u h q -> p h q u"),
                    )
                )
                for engine, low, high in ((nc.vector, 0, VECTOR_ROWS[kind]), (nc.scalar, VECTOR_ROWS[kind], OUT_SIDE)):
                    if high > low:
                        found.append(
                            (
                                engine,
                                out_values[:, low:high, 1 - kind],
                                values[:, :, low:high, 0:PAIRS, :].rearrange("p u h q t -> p h q u t"),
                            )
                        )
            else:
                base = SHIFT + place * PAIR
                values = (
                    tile[:]
                    .rearrange("p (t y) -> p t y", t=2)[:, :, base : base + PAIR]
                    .rearrange("p t (u y) -> p t u y", u=2)[:, :, :, 0:ROW]
                    .rearrange("p t u (h w r) -> p t u h w r", w=SIDE // 2, r=2)
                )
                for engine, low, high in ((nc.vector, 0, VECTOR_ROWS[kind]), (nc.scalar, VECTOR_ROWS[kind], OUT_SIDE)):
                    if high > low:
                        found.append(
                            (
                                engine,
                                out_values[:, low:high].rearrange("p h r q u t -> p h q r u t"),
                                values[:, :, :, low:high, 0:PAIRS, :].rearrange("p t u h q r -> p h q r u t"),
                            )
                        )
            return found

        def regroup(unit):
            grouped = groups.tile([P, 4 * POSITIONS], BF16, align_bytes=64, name="grouped")
            for engine, to, source in pieces(unit, grouped):
                if engine is nc.vector:
                    nc.vector.tensor_copy(out=to, in_=source)
                else:
                    nc.scalar.copy(out=to, in_=source)
            grouped_of_unit[unit] = grouped

        def quantise(unit):
            calls = HALVES if unit == len(units) - 1 else 1
            width = POSITIONS // calls
            quantised_of_unit[unit] = []
            for call in range(calls):
                codes = quantised.tile([P, width], U32, align_bytes=64, name="codes")
                scales = quantised.tile([P, width], U8, align_bytes=64, name="scales")
                nc.vector.quantize_mx(
                    out=codes[:].bitcast(FP8X4),
                    scales=scales[:],
                    in_=grouped_of_unit[unit][:, 4 * width * call : 4 * width * (call + 1)],
                )
                for first in range(0, width, N_TILE):
                    quantised_of_unit[unit].append((codes[:, first : first + N_TILE], scales[:, first : first + N_TILE]))

        def multiply(unit):
            z, kind, n = units[unit]
            slot = (0, 1, 3)[kind]
            for half in range(HALVES):
                codes, scales = quantised_of_unit[unit][half]
                for block in range(MASKS):
                    nc.tensor.matmul_mx(
                        out=acc[n][half][:],
                        lhsT=w_words[:, z, block, slot, :].bitcast(FP4X4),
                        lhsT_scale=w_scales[:, z, block, :],
                        rhs=codes.bitcast(FP8X4),
                        rhs_scale=scales,
                        start=(z == 0 and kind == 0 and block == 0),
                        stop=(z == SETS - 1 and kind == KINDS - 1 and block == MASKS - 1),
                    )

        def add_bias_and_store(n):
            out_rows = out[n].rearrange("o p q -> o (p q)")
            for half in range(HALVES):
                columns = slice(half * N_TILE, (half + 1) * N_TILE)
                result = results.tile([OUT_CHANNELS, N_TILE], F32, name="result")
                nc.scalar.activation(
                    out=result[:].rearrange("o (h q r) -> o h q r", h=HALF_ROWS, r=2),
                    in_=acc[n][half][:].rearrange("o (h r q) -> o h q r", h=HALF_ROWS, r=2),
                    func=mybir.ActivationFunctionType.Identity,
                    bias=bias_f32[:, 0:1],
                )
                nc.scalar.dma_start(out=out_rows[:, columns], in_=result[:])

        moves_before_unit = {
            0: ((3, 0, 0, 1), (0, 1, 1, 1)),
            1: ((1, 1, 2, 1),),
            2: ((3, 1, 2, 0),),
        }
        with tc.manual_schedule():
            for z in range(SETS):
                for members in TILE_IMAGES[z]:
                    if z == 0 and members[0] == 0:
                        load_rows(z, members, (nc.sync, nc.scalar))
                        load_weight()
                    else:
                        load_rows(z, members, (nc.sync, nc.sync))
            for turn in range(len(units) + 3):
                if turn < len(units):
                    regroup(turn)
                if 1 <= turn <= len(units):
                    quantise(turn - 1)
                    for move in moves_before_unit.get(turn - 1, ()):
                        move_bytes(move[0], move[1], move[2], move[3])
                    multiply(turn - 1)
                if turn >= 3 and units[turn - 3][0] == SETS - 1 and units[turn - 3][1] == KINDS - 1:
                    add_bias_and_store(units[turn - 3][2])
